import numpy as np
import ml_dtypes

BF16 = ml_dtypes.bfloat16


def bf(x):
    return np.asarray(x, np.float32).astype(BF16)


def f32(x):
    return np.asarray(x, np.float32)


def f64(x):
    return np.asarray(x).astype(np.float64)


def striped(idx):
    return np.tile(idx.reshape(-1, 16).T, (8, 1))


D, S, KN, M, N, H = 128, 1024, 8, 128, 8192, 512
EPS = 1e-5


def setup_inputs():
    idx = np.concatenate([np.random.permutation(S)[:H] for _ in range(N // H)])
    return {"x": bf(np.random.standard_normal((D, S))), "w_nb": bf(np.random.standard_normal((D, M)) / np.sqrt(D)), "w_ctr": bf(np.random.standard_normal((D, M)) / np.sqrt(D)), "gamma": f32(1.0 + 0.1 * np.random.standard_normal((M, 1))), "beta": f32(0.1 * np.random.standard_normal((M, 1))), "offs": striped(idx)}


def reference(x, w_nb, w_ctr, gamma, beta, offs):
    idx = offs[:16].T.reshape(-1)
    xf = f64(x)
    y = f64(w_nb).T @ xf[:, idx]
    ctr = f64(w_ctr).T @ xf - f64(w_nb).T @ xf
    e = y.reshape(M, S, KN).max(axis=-1) + ctr
    mean = e.mean(axis=1, keepdims=True)
    var = np.square(e - mean).mean(axis=1, keepdims=True)
    return (e - mean) / np.sqrt(var + EPS) * f64(gamma) + f64(beta)

@@ -1,0 +1,93 @@
+import concourse.mybir as mybir
+
+BF16 = mybir.dt.bfloat16
+F32 = mybir.dt.float32
+U16 = mybir.dt.uint16
+ALU = mybir.AluOpType
+ACT = mybir.ActivationFunctionType
+AXIS_X = mybir.AxisListType.X
+
+D = 128
+M = 128
+S = 1024
+KN = 8
+N = S * KN
+PIECE = 512
+PIECE_NODES = PIECE // KN
+PIECE_COLS = PIECE // 16
+BANK = 512
+EPS = 1e-5
+
+FLOPS = 2 * D * M * (N + 2 * S)
+
+
+def tile_spiralconvcombined_kernel(tc, x, w_nb, w_ctr, gamma, beta, offs, out):
+    nc = tc.nc
+    with (
+        tc.tile_pool(name="held", bufs=1) as held,
+        tc.psum_pool(name="ctr_banks", bufs=1) as ctr_banks,
+        tc.psum_pool(name="y_banks", bufs=4) as y_banks,
+    ):
+        x_sb = held.tile([D, S], BF16, name="x_sb")
+        nc.scalar.dma_start(x_sb[:], x)
+        w_nb_sb = held.tile([D, M], BF16, name="w_nb_sb")
+        nc.sync.dma_start(w_nb_sb[:], w_nb)
+        w_ctr_sb = held.tile([D, M], BF16, name="w_ctr_sb")
+        nc.sync.dma_start(w_ctr_sb[:], w_ctr)
+        offsets = held.tile([128, N // 16], U16, name="offsets")
+        nc.sync.dma_start(offsets[:], offs)
+        gamma_sb = held.tile([M, 1], F32, name="gamma_sb")
+        nc.scalar.dma_start(gamma_sb[:], gamma)
+        beta_sb = held.tile([M, 1], F32, name="beta_sb")
+        nc.scalar.dma_start(beta_sb[:], beta)
+
+        eps_sb = held.tile([M, 1], F32, name="eps_sb")
+        nc.vector.memset(eps_sb[:], EPS)
+
+        w_nb_neg = held.tile([D, M], BF16, name="w_nb_neg")
+        nc.vector.tensor_scalar_mul(w_nb_neg[:], w_nb_sb[:], -1.0)
+        ctr = []
+        for h in range(S // BANK):
+            nodes = slice(h * BANK, (h + 1) * BANK)
+            ctr_h = ctr_banks.tile([M, BANK], F32, name=f"ctr{h}")
+            nc.tensor.matmul(ctr_h[:], w_ctr_sb[:], x_sb[:, nodes], start=True, stop=False)
+            nc.tensor.matmul(ctr_h[:], w_nb_neg[:], x_sb[:, nodes], start=False, stop=True)
+            ctr.append(ctr_h)
+
+        peak = held.tile([M, S], F32, name="peak")
+        for r in range(N // PIECE):
+            y = y_banks.tile([M, PIECE], F32, name="y")
+            piece = offsets[:, r * PIECE_COLS : (r + 1) * PIECE_COLS]
+            nc.tensor.matmul(y[:], w_nb_sb[:], x_sb[:].indirect(piece), start=True, stop=True)
+            nc.vector.tensor_reduce(
+                out=peak[:, r * PIECE_NODES : (r + 1) * PIECE_NODES],
+                in_=y[:].rearrange("m (n t) -> m n t", t=KN),
+                axis=AXIS_X,
+                op=ALU.max,
+            )
+
+        e = held.tile([M, S], F32, name="e")
+        stats = held.tile([M, (S // BANK) * 6], F32, name="stats")
+        for h in range(S // BANK):
+            nodes = slice(h * BANK, (h + 1) * BANK)
+            nc.vector.tensor_tensor(e[:, nodes], peak[:, nodes], ctr[h][:], ALU.add)
+            nc.vector.bn_stats(stats[:, h * 6 : (h + 1) * 6], e[:, nodes])
+        mean_var = held.tile([M, 2], F32, name="mean_var")
+        nc.vector.bn_aggr(mean_var[:], stats[:])
+
+        std = held.tile([M, 1], F32, name="std")
+        nc.scalar.activation(std[:], mean_var[:, 1:2], ACT.Sqrt, bias=eps_sb[:])
+        rstd = held.tile([M, 1], F32, name="rstd")
+        nc.vector.reciprocal(rstd[:], std[:])
+        scale = held.tile([M, 1], F32, name="scale")
+        nc.vector.tensor_mul(scale[:], gamma_sb[:], rstd[:])
+        mean_scaled = held.tile([M, 1], F32, name="mean_scaled")
+        nc.vector.tensor_mul(mean_scaled[:], mean_var[:, 0:1], scale[:])
+        shift = held.tile([M, 1], F32, name="shift")
+        nc.vector.tensor_sub(shift[:], beta_sb[:], mean_scaled[:])
+
+        result = held.tile([M, S], F32, name="result")
+        nc.vector.tensor_scalar(result[:, :BANK], e[:, :BANK], scale[:], shift[:], ALU.mult, ALU.add)
+        nc.sync.dma_start(out[:, :BANK], result[:, :BANK])
+        nc.scalar.activation(result[:, BANK:], e[:, BANK:], ACT.Identity, bias=shift[:], scale=scale[:])
+        nc.scalar.dma_start(out[:, BANK:], result[:, BANK:])

@@ -16,6 +16,8 @@ PIECE = 512
 PIECE_NODES = PIECE // KN
 PIECE_COLS = PIECE // 16
 BANK = 512
+CHUNK_PIECES = (4, 4, 4, 3, 1)
+BLOCK = 256
 EPS = 1e-5
 
 FLOPS = 2 * D * M * (N + 2 * S)
@@ -43,51 +45,64 @@ def tile_spiralconvcombined_kernel(tc, x, w_nb, w_ctr, gamma, beta, offs, out):
 
         eps_sb = held.tile([M, 1], F32, name="eps_sb")
         nc.vector.memset(eps_sb[:], EPS)
+        scratch = held.tile([M, 1], F32, name="scratch")
+        nc.scalar.activation(scratch[:], eps_sb[:], ACT.Sqrt)
 
         w_nb_neg = held.tile([D, M], BF16, name="w_nb_neg")
         nc.vector.tensor_scalar_mul(w_nb_neg[:], w_nb_sb[:], -1.0)
-        ctr = []
+        ctr_sb = held.tile([M, S], F32, name="ctr_sb")
         for h in range(S // BANK):
             nodes = slice(h * BANK, (h + 1) * BANK)
-            ctr_h = ctr_banks.tile([M, BANK], F32, name=f"ctr{h}")
-            nc.tensor.matmul(ctr_h[:], w_ctr_sb[:], x_sb[:, nodes], start=True, stop=False)
-            nc.tensor.matmul(ctr_h[:], w_nb_neg[:], x_sb[:, nodes], start=False, stop=True)
-            ctr.append(ctr_h)
+            ctr_ps = ctr_banks.tile([M, BANK], F32, name=f"ctr_ps{h}")
+            nc.tensor.matmul(ctr_ps[:], w_ctr_sb[:], x_sb[:, nodes], start=True, stop=False)
+            nc.tensor.matmul(ctr_ps[:], w_nb_neg[:], x_sb[:, nodes], start=False, stop=True)
+            nc.scalar.copy(ctr_sb[:, nodes], ctr_ps[:])
+
+        neg_gamma = held.tile([M, 1], F32, name="neg_gamma")
+        nc.gpsimd.tensor_scalar_mul(neg_gamma[:], gamma_sb[:], -1.0)
 
         peak = held.tile([M, S], F32, name="peak")
-        for r in range(N // PIECE):
-            y = y_banks.tile([M, PIECE], F32, name="y")
-            piece = offsets[:, r * PIECE_COLS : (r + 1) * PIECE_COLS]
-            nc.tensor.matmul(y[:], w_nb_sb[:], x_sb[:].indirect(piece), start=True, stop=True)
-            nc.vector.tensor_reduce(
-                out=peak[:, r * PIECE_NODES : (r + 1) * PIECE_NODES],
-                in_=y[:].rearrange("m (n t) -> m n t", t=KN),
-                axis=AXIS_X,
-                op=ALU.max,
-            )
-
         e = held.tile([M, S], F32, name="e")
-        stats = held.tile([M, (S // BANK) * 6], F32, name="stats")
-        for h in range(S // BANK):
-            nodes = slice(h * BANK, (h + 1) * BANK)
-            nc.vector.tensor_tensor(e[:, nodes], peak[:, nodes], ctr[h][:], ALU.add)
-            nc.vector.bn_stats(stats[:, h * 6 : (h + 1) * 6], e[:, nodes])
+        stats = held.tile([M, len(CHUNK_PIECES) * 6], F32, name="stats")
+        last_chunk = len(CHUNK_PIECES) - 1
+        first_piece = 0
+        for c, n_pieces in enumerate(CHUNK_PIECES):
+            for r in range(first_piece, first_piece + n_pieces):
+                y = y_banks.tile([M, PIECE], F32, name="y")
+                piece = offsets[:, r * PIECE_COLS : (r + 1) * PIECE_COLS]
+                nc.tensor.matmul(y[:], w_nb_sb[:], x_sb[:].indirect(piece), start=True, stop=True)
+                nc.vector.tensor_reduce(
+                    out=peak[:, r * PIECE_NODES : (r + 1) * PIECE_NODES],
+                    in_=y[:].rearrange("m (n t) -> m n t", t=KN),
+                    axis=AXIS_X,
+                    op=ALU.max,
+                )
+            nodes = slice(first_piece * PIECE_NODES, (first_piece + n_pieces) * PIECE_NODES)
+            adder = nc.vector if c == last_chunk else nc.gpsimd
+            adder.tensor_tensor(e[:, nodes], peak[:, nodes], ctr_sb[:, nodes], ALU.add)
+            nc.vector.bn_stats(stats[:, c * 6 : (c + 1) * 6], e[:, nodes])
+            first_piece += n_pieces
+
         mean_var = held.tile([M, 2], F32, name="mean_var")
         nc.vector.bn_aggr(mean_var[:], stats[:])
-
         std = held.tile([M, 1], F32, name="std")
         nc.scalar.activation(std[:], mean_var[:, 1:2], ACT.Sqrt, bias=eps_sb[:])
+        neg_mean_gamma = held.tile([M, 1], F32, name="neg_mean_gamma")
+        nc.vector.tensor_mul(neg_mean_gamma[:], mean_var[:, 0:1], neg_gamma[:])
         rstd = held.tile([M, 1], F32, name="rstd")
         nc.vector.reciprocal(rstd[:], std[:])
         scale = held.tile([M, 1], F32, name="scale")
         nc.vector.tensor_mul(scale[:], gamma_sb[:], rstd[:])
-        mean_scaled = held.tile([M, 1], F32, name="mean_scaled")
-        nc.vector.tensor_mul(mean_scaled[:], mean_var[:, 0:1], scale[:])
         shift = held.tile([M, 1], F32, name="shift")
-        nc.vector.tensor_sub(shift[:], beta_sb[:], mean_scaled[:])
+        nc.vector.tensor_scalar(shift[:], neg_mean_gamma[:], rstd[:], beta_sb[:], ALU.mult, ALU.add)
 
         result = held.tile([M, S], F32, name="result")
-        nc.vector.tensor_scalar(result[:, :BANK], e[:, :BANK], scale[:], shift[:], ALU.mult, ALU.add)
-        nc.sync.dma_start(out[:, :BANK], result[:, :BANK])
-        nc.scalar.activation(result[:, BANK:], e[:, BANK:], ACT.Identity, bias=shift[:], scale=scale[:])
-        nc.scalar.dma_start(out[:, BANK:], result[:, BANK:])
+        scalar_nodes = slice(S - BLOCK, S)
+        nc.scalar.activation(
+            result[:, scalar_nodes], e[:, scalar_nodes], ACT.Identity, bias=shift[:], scale=scale[:]
+        )
+        nc.scalar.dma_start(out[:, scalar_nodes], result[:, scalar_nodes])
+        for b in range(S // BLOCK - 1):
+            nodes = slice(b * BLOCK, (b + 1) * BLOCK)
+            nc.vector.tensor_scalar(result[:, nodes], e[:, nodes], scale[:], shift[:], ALU.mult, ALU.add)
+            nc.sync.dma_start(out[:, nodes], result[:, nodes])

@@ -16,8 +16,11 @@ PIECE = 512
 PIECE_NODES = PIECE // KN
 PIECE_COLS = PIECE // 16
 BANK = 512
-CHUNK_PIECES = (4, 4, 4, 3, 1)
+CHUNK_PIECES = 4
+CHUNKS = N // (PIECE * CHUNK_PIECES)
+CHUNK_NODES = CHUNK_PIECES * PIECE_NODES
 BLOCK = 256
+WARM_MATMULS = 4
 EPS = 1e-5
 
 FLOPS = 2 * D * M * (N + 2 * S)
@@ -27,6 +30,7 @@ def tile_spiralconvcombined_kernel(tc, x, w_nb, w_ctr, gamma, beta, offs, out):
     nc = tc.nc
     with (
         tc.tile_pool(name="held", bufs=1) as held,
+        tc.psum_pool(name="warm_bank", bufs=1) as warm_bank,
         tc.psum_pool(name="ctr_banks", bufs=1) as ctr_banks,
         tc.psum_pool(name="y_banks", bufs=4) as y_banks,
     ):
@@ -42,6 +46,12 @@ def tile_spiralconvcombined_kernel(tc, x, w_nb, w_ctr, gamma, beta, offs, out):
         nc.scalar.dma_start(gamma_sb[:], gamma)
         beta_sb = held.tile([M, 1], F32, name="beta_sb")
         nc.scalar.dma_start(beta_sb[:], beta)
+
+        zeros = held.tile([D, BANK], BF16, name="zeros")
+        nc.vector.memset(zeros[:].bitcast(F32), 0.0)
+        warm = warm_bank.tile([M, BANK], F32, name="warm")
+        for w in range(WARM_MATMULS):
+            nc.tensor.matmul(warm[:], zeros[:, :M], zeros[:], start=True, stop=True)
 
         eps_sb = held.tile([M, 1], F32, name="eps_sb")
         nc.vector.memset(eps_sb[:], EPS)
@@ -63,11 +73,9 @@ def tile_spiralconvcombined_kernel(tc, x, w_nb, w_ctr, gamma, beta, offs, out):
 
         peak = held.tile([M, S], F32, name="peak")
         e = held.tile([M, S], F32, name="e")
-        stats = held.tile([M, len(CHUNK_PIECES) * 6], F32, name="stats")
-        last_chunk = len(CHUNK_PIECES) - 1
-        first_piece = 0
-        for c, n_pieces in enumerate(CHUNK_PIECES):
-            for r in range(first_piece, first_piece + n_pieces):
+        stats = held.tile([M, CHUNKS * 6], F32, name="stats")
+        for c in range(CHUNKS):
+            for r in range(c * CHUNK_PIECES, (c + 1) * CHUNK_PIECES):
                 y = y_banks.tile([M, PIECE], F32, name="y")
                 piece = offsets[:, r * PIECE_COLS : (r + 1) * PIECE_COLS]
                 nc.tensor.matmul(y[:], w_nb_sb[:], x_sb[:].indirect(piece), start=True, stop=True)
@@ -77,11 +85,10 @@ def tile_spiralconvcombined_kernel(tc, x, w_nb, w_ctr, gamma, beta, offs, out):
                     axis=AXIS_X,
                     op=ALU.max,
                 )
-            nodes = slice(first_piece * PIECE_NODES, (first_piece + n_pieces) * PIECE_NODES)
-            adder = nc.vector if c == last_chunk else nc.gpsimd
+            nodes = slice(c * CHUNK_NODES, (c + 1) * CHUNK_NODES)
+            adder = nc.vector if c == CHUNKS - 1 else nc.gpsimd
             adder.tensor_tensor(e[:, nodes], peak[:, nodes], ctr_sb[:, nodes], ALU.add)
             nc.vector.bn_stats(stats[:, c * 6 : (c + 1) * 6], e[:, nodes])
-            first_piece += n_pieces
 
         mean_var = held.tile([M, 2], F32, name="mean_var")
         nc.vector.bn_aggr(mean_var[:], stats[:])

@@ -19,7 +19,9 @@ BANK = 512
 CHUNK_PIECES = 4
 CHUNKS = N // (PIECE * CHUNK_PIECES)
 CHUNK_NODES = CHUNK_PIECES * PIECE_NODES
-BLOCK = 256
+SLOT = 8
+BLOCK = 128
+SCALAR_BLOCKS = 2
 WARM_MATMULS = 4
 EPS = 1e-5
 
@@ -30,9 +32,10 @@ def tile_spiralconvcombined_kernel(tc, x, w_nb, w_ctr, gamma, beta, offs, out):
     nc = tc.nc
     with (
         tc.tile_pool(name="held", bufs=1) as held,
+        tc.tile_pool(name="work", bufs=2) as work,
         tc.psum_pool(name="warm_bank", bufs=1) as warm_bank,
         tc.psum_pool(name="ctr_banks", bufs=1) as ctr_banks,
-        tc.psum_pool(name="y_banks", bufs=4) as y_banks,
+        tc.psum_pool(name="y_banks", bufs=5) as y_banks,
     ):
         x_sb = held.tile([D, S], BF16, name="x_sb")
         nc.scalar.dma_start(x_sb[:], x)
@@ -56,7 +59,7 @@ def tile_spiralconvcombined_kernel(tc, x, w_nb, w_ctr, gamma, beta, offs, out):
         eps_sb = held.tile([M, 1], F32, name="eps_sb")
         nc.vector.memset(eps_sb[:], EPS)
         scratch = held.tile([M, 1], F32, name="scratch")
-        nc.scalar.activation(scratch[:], eps_sb[:], ACT.Sqrt)
+        nc.scalar.activation(scratch[:], eps_sb[:], ACT.Abs_reciprocal_sqrt)
 
         w_nb_neg = held.tile([D, M], BF16, name="w_nb_neg")
         nc.vector.tensor_scalar_mul(w_nb_neg[:], w_nb_sb[:], -1.0)
@@ -73,7 +76,10 @@ def tile_spiralconvcombined_kernel(tc, x, w_nb, w_ctr, gamma, beta, offs, out):
 
         peak = held.tile([M, S], F32, name="peak")
         e = held.tile([M, S], F32, name="e")
-        stats = held.tile([M, CHUNKS * 6], F32, name="stats")
+        stats = held.tile([M, CHUNKS + 1, SLOT], F32, name="stats")
+        chunk_count = held.tile([M, CHUNKS - 1, 1], F32, name="chunk_count")
+        nc.vector.memset(chunk_count[:], float(CHUNK_NODES))
+        nc.scalar.copy(stats[:, : CHUNKS - 1, 0:1], chunk_count[:])
         for c in range(CHUNKS):
             for r in range(c * CHUNK_PIECES, (c + 1) * CHUNK_PIECES):
                 y = y_banks.tile([M, PIECE], F32, name="y")
@@ -86,30 +92,37 @@ def tile_spiralconvcombined_kernel(tc, x, w_nb, w_ctr, gamma, beta, offs, out):
                     op=ALU.max,
                 )
             nodes = slice(c * CHUNK_NODES, (c + 1) * CHUNK_NODES)
-            adder = nc.vector if c == CHUNKS - 1 else nc.gpsimd
-            adder.tensor_tensor(e[:, nodes], peak[:, nodes], ctr_sb[:, nodes], ALU.add)
-            nc.vector.bn_stats(stats[:, c * 6 : (c + 1) * 6], e[:, nodes])
+            if c < CHUNKS - 1:
+                nc.gpsimd.tensor_tensor(e[:, nodes], peak[:, nodes], ctr_sb[:, nodes], ALU.add)
+                unused = work.tile([M, CHUNK_NODES], F32, name="unused")
+                total = work.tile([M, 1], F32, name="total")
+                nc.scalar.activation(unused[:], e[:, nodes], ACT.Identity, accum_out=total[:])
+                nc.scalar.mul(stats[:, c, 1:2], total[:], 1.0 / CHUNK_NODES)
+                nc.scalar.activation(
+                    unused[:], e[:, nodes], ACT.Square,
+                    bias=stats[:, c, 1:2], scale=-1.0, accum_out=stats[:, c, 2:3],
+                )
+            else:
+                nc.vector.tensor_tensor(e[:, nodes], peak[:, nodes], ctr_sb[:, nodes], ALU.add)
+                nc.vector.bn_stats(stats[:, c : c + 2, 0:3], e[:, nodes])
 
         mean_var = held.tile([M, 2], F32, name="mean_var")
-        nc.vector.bn_aggr(mean_var[:], stats[:])
-        std = held.tile([M, 1], F32, name="std")
-        nc.scalar.activation(std[:], mean_var[:, 1:2], ACT.Sqrt, bias=eps_sb[:])
+        nc.vector.bn_aggr(mean_var[:], stats[:, :, 0:3])
+        rstd = held.tile([M, 1], F32, name="rstd")
+        nc.scalar.activation(rstd[:], mean_var[:, 1:2], ACT.Abs_reciprocal_sqrt, bias=eps_sb[:])
         neg_mean_gamma = held.tile([M, 1], F32, name="neg_mean_gamma")
         nc.vector.tensor_mul(neg_mean_gamma[:], mean_var[:, 0:1], neg_gamma[:])
-        rstd = held.tile([M, 1], F32, name="rstd")
-        nc.vector.reciprocal(rstd[:], std[:])
         scale = held.tile([M, 1], F32, name="scale")
         nc.vector.tensor_mul(scale[:], gamma_sb[:], rstd[:])
         shift = held.tile([M, 1], F32, name="shift")
         nc.vector.tensor_scalar(shift[:], neg_mean_gamma[:], rstd[:], beta_sb[:], ALU.mult, ALU.add)
 
         result = held.tile([M, S], F32, name="result")
-        scalar_nodes = slice(S - BLOCK, S)
-        nc.scalar.activation(
-            result[:, scalar_nodes], e[:, scalar_nodes], ACT.Identity, bias=shift[:], scale=scale[:]
-        )
-        nc.scalar.dma_start(out[:, scalar_nodes], result[:, scalar_nodes])
-        for b in range(S // BLOCK - 1):
+        for b in range(S // BLOCK):
             nodes = slice(b * BLOCK, (b + 1) * BLOCK)
-            nc.vector.tensor_scalar(result[:, nodes], e[:, nodes], scale[:], shift[:], ALU.mult, ALU.add)
-            nc.sync.dma_start(out[:, nodes], result[:, nodes])
+            if b < SCALAR_BLOCKS:
+                nc.scalar.activation(result[:, nodes], e[:, nodes], ACT.Identity, bias=shift[:], scale=scale[:])
+                nc.scalar.dma_start(out[:, nodes], result[:, nodes])
+            else:
+                nc.vector.tensor_scalar(result[:, nodes], e[:, nodes], scale[:], shift[:], ALU.mult, ALU.add)
+                nc.sync.dma_start(out[:, nodes], result[:, nodes])

@@ -16,9 +16,8 @@ PIECE = 512
 PIECE_NODES = PIECE // KN
 PIECE_COLS = PIECE // 16
 BANK = 512
-CHUNK_PIECES = 4
-CHUNKS = N // (PIECE * CHUNK_PIECES)
-CHUNK_NODES = CHUNK_PIECES * PIECE_NODES
+CHUNK_PIECES = (4, 4, 4, 2, 2)
+CHUNKS = len(CHUNK_PIECES)
 SLOT = 8
 BLOCK = 128
 SCALAR_BLOCKS = 2
@@ -78,10 +77,13 @@ def tile_spiralconvcombined_kernel(tc, x, w_nb, w_ctr, gamma, beta, offs, out):
         e = held.tile([M, S], F32, name="e")
         stats = held.tile([M, CHUNKS + 1, SLOT], F32, name="stats")
         chunk_count = held.tile([M, CHUNKS - 1, 1], F32, name="chunk_count")
-        nc.vector.memset(chunk_count[:], float(CHUNK_NODES))
+        for c in range(CHUNKS - 1):
+            nc.vector.memset(chunk_count[:, c, :], float(CHUNK_PIECES[c] * PIECE_NODES))
         nc.scalar.copy(stats[:, : CHUNKS - 1, 0:1], chunk_count[:])
         for c in range(CHUNKS):
-            for r in range(c * CHUNK_PIECES, (c + 1) * CHUNK_PIECES):
+            first_piece = sum(CHUNK_PIECES[:c])
+            chunk_nodes = CHUNK_PIECES[c] * PIECE_NODES
+            for r in range(first_piece, first_piece + CHUNK_PIECES[c]):
                 y = y_banks.tile([M, PIECE], F32, name="y")
                 piece = offsets[:, r * PIECE_COLS : (r + 1) * PIECE_COLS]
                 nc.tensor.matmul(y[:], w_nb_sb[:], x_sb[:].indirect(piece), start=True, stop=True)
@@ -91,13 +93,13 @@ def tile_spiralconvcombined_kernel(tc, x, w_nb, w_ctr, gamma, beta, offs, out):
                     axis=AXIS_X,
                     op=ALU.max,
                 )
-            nodes = slice(c * CHUNK_NODES, (c + 1) * CHUNK_NODES)
+            nodes = slice(first_piece * PIECE_NODES, first_piece * PIECE_NODES + chunk_nodes)
             if c < CHUNKS - 1:
                 nc.gpsimd.tensor_tensor(e[:, nodes], peak[:, nodes], ctr_sb[:, nodes], ALU.add)
-                unused = work.tile([M, CHUNK_NODES], F32, name="unused")
+                unused = work.tile([M, chunk_nodes], F32, name="unused")
                 total = work.tile([M, 1], F32, name="total")
                 nc.scalar.activation(unused[:], e[:, nodes], ACT.Identity, accum_out=total[:])
-                nc.scalar.mul(stats[:, c, 1:2], total[:], 1.0 / CHUNK_NODES)
+                nc.scalar.mul(stats[:, c, 1:2], total[:], 1.0 / chunk_nodes)
                 nc.scalar.activation(
                     unused[:], e[:, nodes], ACT.Square,
                     bias=stats[:, c, 1:2], scale=-1.0, accum_out=stats[:, c, 2:3],
@@ -122,7 +124,7 @@ def tile_spiralconvcombined_kernel(tc, x, w_nb, w_ctr, gamma, beta, offs, out):
             nodes = slice(b * BLOCK, (b + 1) * BLOCK)
             if b < SCALAR_BLOCKS:
                 nc.scalar.activation(result[:, nodes], e[:, nodes], ACT.Identity, bias=shift[:], scale=scale[:])
-                nc.scalar.dma_start(out[:, nodes], result[:, nodes])
             else:
                 nc.vector.tensor_scalar(result[:, nodes], e[:, nodes], scale[:], shift[:], ALU.mult, ALU.add)
-                nc.sync.dma_start(out[:, nodes], result[:, nodes])
+            store_queue = nc.sync if b % 2 == 0 else nc.scalar
+            store_queue.dma_start(out[:, nodes], result[:, nodes])

@@ -16,12 +16,13 @@ PIECE = 512
 PIECE_NODES = PIECE // KN
 PIECE_COLS = PIECE // 16
 BANK = 512
-CHUNK_PIECES = (4, 4, 4, 2, 2)
-CHUNKS = len(CHUNK_PIECES)
+CHUNK_PIECES = 4
+CHUNKS = N // (PIECE * CHUNK_PIECES)
+CHUNK_NODES = CHUNK_PIECES * PIECE_NODES
 SLOT = 8
 BLOCK = 128
 SCALAR_BLOCKS = 2
-WARM_MATMULS = 4
+WARM_MATMULS = 2
 EPS = 1e-5
 
 FLOPS = 2 * D * M * (N + 2 * S)
@@ -77,13 +78,10 @@ def tile_spiralconvcombined_kernel(tc, x, w_nb, w_ctr, gamma, beta, offs, out):
         e = held.tile([M, S], F32, name="e")
         stats = held.tile([M, CHUNKS + 1, SLOT], F32, name="stats")
         chunk_count = held.tile([M, CHUNKS - 1, 1], F32, name="chunk_count")
-        for c in range(CHUNKS - 1):
-            nc.vector.memset(chunk_count[:, c, :], float(CHUNK_PIECES[c] * PIECE_NODES))
+        nc.vector.memset(chunk_count[:], float(CHUNK_NODES))
         nc.scalar.copy(stats[:, : CHUNKS - 1, 0:1], chunk_count[:])
         for c in range(CHUNKS):
-            first_piece = sum(CHUNK_PIECES[:c])
-            chunk_nodes = CHUNK_PIECES[c] * PIECE_NODES
-            for r in range(first_piece, first_piece + CHUNK_PIECES[c]):
+            for r in range(c * CHUNK_PIECES, (c + 1) * CHUNK_PIECES):
                 y = y_banks.tile([M, PIECE], F32, name="y")
                 piece = offsets[:, r * PIECE_COLS : (r + 1) * PIECE_COLS]
                 nc.tensor.matmul(y[:], w_nb_sb[:], x_sb[:].indirect(piece), start=True, stop=True)
@@ -93,13 +91,13 @@ def tile_spiralconvcombined_kernel(tc, x, w_nb, w_ctr, gamma, beta, offs, out):
                     axis=AXIS_X,
                     op=ALU.max,
                 )
-            nodes = slice(first_piece * PIECE_NODES, first_piece * PIECE_NODES + chunk_nodes)
+            nodes = slice(c * CHUNK_NODES, (c + 1) * CHUNK_NODES)
             if c < CHUNKS - 1:
                 nc.gpsimd.tensor_tensor(e[:, nodes], peak[:, nodes], ctr_sb[:, nodes], ALU.add)
-                unused = work.tile([M, chunk_nodes], F32, name="unused")
+                unused = work.tile([M, CHUNK_NODES], F32, name="unused")
                 total = work.tile([M, 1], F32, name="total")
                 nc.scalar.activation(unused[:], e[:, nodes], ACT.Identity, accum_out=total[:])
-                nc.scalar.mul(stats[:, c, 1:2], total[:], 1.0 / chunk_nodes)
+                nc.scalar.mul(stats[:, c, 1:2], total[:], 1.0 / CHUNK_NODES)
                 nc.scalar.activation(
                     unused[:], e[:, nodes], ACT.Square,
                     bias=stats[:, c, 1:2], scale=-1.0, accum_out=stats[:, c, 2:3],
@@ -124,7 +122,7 @@ def tile_spiralconvcombined_kernel(tc, x, w_nb, w_ctr, gamma, beta, offs, out):
             nodes = slice(b * BLOCK, (b + 1) * BLOCK)
             if b < SCALAR_BLOCKS:
                 nc.scalar.activation(result[:, nodes], e[:, nodes], ACT.Identity, bias=shift[:], scale=scale[:])
+                nc.scalar.dma_start(out[:, nodes], result[:, nodes])
             else:
                 nc.vector.tensor_scalar(result[:, nodes], e[:, nodes], scale[:], shift[:], ALU.mult, ALU.add)
-            store_queue = nc.sync if b % 2 == 0 else nc.scalar
-            store_queue.dma_start(out[:, nodes], result[:, nodes])
+                nc.sync.dma_start(out[:, nodes], result[:, nodes])

@@ -22,7 +22,7 @@ CHUNK_NODES = CHUNK_PIECES * PIECE_NODES
 SLOT = 8
 BLOCK = 128
 SCALAR_BLOCKS = 2
-WARM_MATMULS = 2
+WARM_MATMULS = 4
 EPS = 1e-5
 
 FLOPS = 2 * D * M * (N + 2 * S)
@@ -59,7 +59,7 @@ def tile_spiralconvcombined_kernel(tc, x, w_nb, w_ctr, gamma, beta, offs, out):
         eps_sb = held.tile([M, 1], F32, name="eps_sb")
         nc.vector.memset(eps_sb[:], EPS)
         scratch = held.tile([M, 1], F32, name="scratch")
-        nc.scalar.activation(scratch[:], eps_sb[:], ACT.Abs_reciprocal_sqrt)
+        nc.scalar.activation(scratch[:], eps_sb[:], ACT.Sqrt)
 
         w_nb_neg = held.tile([D, M], BF16, name="w_nb_neg")
         nc.vector.tensor_scalar_mul(w_nb_neg[:], w_nb_sb[:], -1.0)
@@ -108,10 +108,12 @@ def tile_spiralconvcombined_kernel(tc, x, w_nb, w_ctr, gamma, beta, offs, out):
 
         mean_var = held.tile([M, 2], F32, name="mean_var")
         nc.vector.bn_aggr(mean_var[:], stats[:, :, 0:3])
-        rstd = held.tile([M, 1], F32, name="rstd")
-        nc.scalar.activation(rstd[:], mean_var[:, 1:2], ACT.Abs_reciprocal_sqrt, bias=eps_sb[:])
+        std = held.tile([M, 1], F32, name="std")
+        nc.scalar.activation(std[:], mean_var[:, 1:2], ACT.Sqrt, bias=eps_sb[:])
         neg_mean_gamma = held.tile([M, 1], F32, name="neg_mean_gamma")
         nc.vector.tensor_mul(neg_mean_gamma[:], mean_var[:, 0:1], neg_gamma[:])
+        rstd = held.tile([M, 1], F32, name="rstd")
+        nc.vector.reciprocal(rstd[:], std[:])
         scale = held.tile([M, 1], F32, name="scale")
         nc.vector.tensor_mul(scale[:], gamma_sb[:], rstd[:])
         shift = held.tile([M, 1], F32, name="shift")

@@ -22,7 +22,8 @@ CHUNK_NODES = CHUNK_PIECES * PIECE_NODES
 SLOT = 8
 BLOCK = 128
 SCALAR_BLOCKS = 2
-WARM_MATMULS = 4
+WARM_MATMULS = 3
+QUARTER = 256
 EPS = 1e-5
 
 FLOPS = 2 * D * M * (N + 2 * S)
@@ -37,12 +38,15 @@ def tile_spiralconvcombined_kernel(tc, x, w_nb, w_ctr, gamma, beta, offs, out):
         tc.psum_pool(name="ctr_banks", bufs=1) as ctr_banks,
         tc.psum_pool(name="y_banks", bufs=5) as y_banks,
     ):
-        x_sb = held.tile([D, S], BF16, name="x_sb")
-        nc.scalar.dma_start(x_sb[:], x)
         w_nb_sb = held.tile([D, M], BF16, name="w_nb_sb")
         nc.sync.dma_start(w_nb_sb[:], w_nb)
         w_ctr_sb = held.tile([D, M], BF16, name="w_ctr_sb")
-        nc.sync.dma_start(w_ctr_sb[:], w_ctr)
+        nc.scalar.dma_start(w_ctr_sb[:], w_ctr)
+        x_sb = held.tile([D, S], BF16, name="x_sb")
+        for q in range(S // QUARTER):
+            nodes = slice(q * QUARTER, (q + 1) * QUARTER)
+            load_queue = nc.sync if q % 2 == 0 else nc.scalar
+            load_queue.dma_start(x_sb[:, nodes], x[:, nodes])
         offsets = held.tile([128, N // 16], U16, name="offsets")
         nc.sync.dma_start(offsets[:], offs)
         gamma_sb = held.tile([M, 1], F32, name="gamma_sb")
@@ -59,17 +63,19 @@ def tile_spiralconvcombined_kernel(tc, x, w_nb, w_ctr, gamma, beta, offs, out):
         eps_sb = held.tile([M, 1], F32, name="eps_sb")
         nc.vector.memset(eps_sb[:], EPS)
         scratch = held.tile([M, 1], F32, name="scratch")
-        nc.scalar.activation(scratch[:], eps_sb[:], ACT.Sqrt)
+        nc.scalar.activation(scratch[:], eps_sb[:], ACT.Abs_reciprocal_sqrt)
 
         w_nb_neg = held.tile([D, M], BF16, name="w_nb_neg")
         nc.vector.tensor_scalar_mul(w_nb_neg[:], w_nb_sb[:], -1.0)
         ctr_sb = held.tile([M, S], F32, name="ctr_sb")
         for h in range(S // BANK):
-            nodes = slice(h * BANK, (h + 1) * BANK)
             ctr_ps = ctr_banks.tile([M, BANK], F32, name=f"ctr_ps{h}")
-            nc.tensor.matmul(ctr_ps[:], w_ctr_sb[:], x_sb[:, nodes], start=True, stop=False)
-            nc.tensor.matmul(ctr_ps[:], w_nb_neg[:], x_sb[:, nodes], start=False, stop=True)
-            nc.scalar.copy(ctr_sb[:, nodes], ctr_ps[:])
+            for q in range(BANK // QUARTER):
+                cols = slice(q * QUARTER, (q + 1) * QUARTER)
+                nodes = slice(h * BANK + q * QUARTER, h * BANK + (q + 1) * QUARTER)
+                nc.tensor.matmul(ctr_ps[:, cols], w_ctr_sb[:], x_sb[:, nodes], start=True, stop=False)
+                nc.tensor.matmul(ctr_ps[:, cols], w_nb_neg[:], x_sb[:, nodes], start=False, stop=True)
+            nc.scalar.copy(ctr_sb[:, h * BANK : (h + 1) * BANK], ctr_ps[:])
 
         neg_gamma = held.tile([M, 1], F32, name="neg_gamma")
         nc.gpsimd.tensor_scalar_mul(neg_gamma[:], gamma_sb[:], -1.0)
@@ -108,12 +114,10 @@ def tile_spiralconvcombined_kernel(tc, x, w_nb, w_ctr, gamma, beta, offs, out):
 
         mean_var = held.tile([M, 2], F32, name="mean_var")
         nc.vector.bn_aggr(mean_var[:], stats[:, :, 0:3])
-        std = held.tile([M, 1], F32, name="std")
-        nc.scalar.activation(std[:], mean_var[:, 1:2], ACT.Sqrt, bias=eps_sb[:])
+        rstd = held.tile([M, 1], F32, name="rstd")
+        nc.scalar.activation(rstd[:], mean_var[:, 1:2], ACT.Abs_reciprocal_sqrt, bias=eps_sb[:])
         neg_mean_gamma = held.tile([M, 1], F32, name="neg_mean_gamma")
         nc.vector.tensor_mul(neg_mean_gamma[:], mean_var[:, 0:1], neg_gamma[:])
-        rstd = held.tile([M, 1], F32, name="rstd")
-        nc.vector.reciprocal(rstd[:], std[:])
         scale = held.tile([M, 1], F32, name="scale")
         nc.vector.tensor_mul(scale[:], gamma_sb[:], rstd[:])
         shift = held.tile([M, 1], F32, name="shift")

@@ -67,15 +67,21 @@ def tile_spiralconvcombined_kernel(tc, x, w_nb, w_ctr, gamma, beta, offs, out):
 
         w_nb_neg = held.tile([D, M], BF16, name="w_nb_neg")
         nc.vector.tensor_scalar_mul(w_nb_neg[:], w_nb_sb[:], -1.0)
-        ctr_sb = held.tile([M, S], F32, name="ctr_sb")
-        for h in range(S // BANK):
-            ctr_ps = ctr_banks.tile([M, BANK], F32, name=f"ctr_ps{h}")
-            for q in range(BANK // QUARTER):
-                cols = slice(q * QUARTER, (q + 1) * QUARTER)
-                nodes = slice(h * BANK + q * QUARTER, h * BANK + (q + 1) * QUARTER)
-                nc.tensor.matmul(ctr_ps[:, cols], w_ctr_sb[:], x_sb[:, nodes], start=True, stop=False)
-                nc.tensor.matmul(ctr_ps[:, cols], w_nb_neg[:], x_sb[:, nodes], start=False, stop=True)
-            nc.scalar.copy(ctr_sb[:, h * BANK : (h + 1) * BANK], ctr_ps[:])
+        def ctr_matmuls(ctr_cols, nodes):
+            nc.tensor.matmul(ctr_cols, w_ctr_sb[:], x_sb[:, nodes], start=True, stop=False)
+            nc.tensor.matmul(ctr_cols, w_nb_neg[:], x_sb[:, nodes], start=False, stop=True)
+
+        early_nodes = (CHUNKS - 1) * CHUNK_NODES
+        ctr_sb = held.tile([M, early_nodes], F32, name="ctr_sb")
+        for first in range(0, early_nodes, BANK):
+            width = min(BANK, early_nodes - first)
+            ctr_ps = ctr_banks.tile([M, BANK], F32, name=f"ctr_ps{first // BANK}")
+            for q in range(width // QUARTER):
+                ctr_matmuls(
+                    ctr_ps[:, q * QUARTER : (q + 1) * QUARTER],
+                    slice(first + q * QUARTER, first + (q + 1) * QUARTER),
+                )
+            nc.scalar.copy(ctr_sb[:, first : first + width], ctr_ps[:, :width])
 
         neg_gamma = held.tile([M, 1], F32, name="neg_gamma")
         nc.gpsimd.tensor_scalar_mul(neg_gamma[:], gamma_sb[:], -1.0)
@@ -109,7 +115,9 @@ def tile_spiralconvcombined_kernel(tc, x, w_nb, w_ctr, gamma, beta, offs, out):
                     bias=stats[:, c, 1:2], scale=-1.0, accum_out=stats[:, c, 2:3],
                 )
             else:
-                nc.vector.tensor_tensor(e[:, nodes], peak[:, nodes], ctr_sb[:, nodes], ALU.add)
+                ctr_last = y_banks.tile([M, PIECE], F32, name="ctr_last", tag="y")
+                ctr_matmuls(ctr_last[:, :CHUNK_NODES], nodes)
+                nc.vector.tensor_tensor(e[:, nodes], peak[:, nodes], ctr_last[:, :CHUNK_NODES], ALU.add)
                 nc.vector.bn_stats(stats[:, c : c + 2, 0:3], e[:, nodes])
 
         mean_var = held.tile([M, 2], F32, name="mean_var")

@@ -20,8 +20,8 @@ CHUNK_PIECES = 4
 CHUNKS = N // (PIECE * CHUNK_PIECES)
 CHUNK_NODES = CHUNK_PIECES * PIECE_NODES
 SLOT = 8
-BLOCK = 128
-SCALAR_BLOCKS = 2
+BLOCK = 256
+SCALAR_BLOCKS = 1
 WARM_MATMULS = 3
 QUARTER = 256
 EPS = 1e-5

@@ -88,7 +88,7 @@ def tile_spiralconvcombined_kernel(tc, x, w_nb, w_ctr, gamma, beta, offs, out):
 
         peak = held.tile([M, S], F32, name="peak")
         e = held.tile([M, S], F32, name="e")
-        stats = held.tile([M, CHUNKS + 1, SLOT], F32, name="stats")
+        stats = held.tile([M, CHUNKS + 3, SLOT], F32, name="stats")
         chunk_count = held.tile([M, CHUNKS - 1, 1], F32, name="chunk_count")
         nc.vector.memset(chunk_count[:], float(CHUNK_NODES))
         nc.scalar.copy(stats[:, : CHUNKS - 1, 0:1], chunk_count[:])
@@ -117,8 +117,14 @@ def tile_spiralconvcombined_kernel(tc, x, w_nb, w_ctr, gamma, beta, offs, out):
             else:
                 ctr_last = y_banks.tile([M, PIECE], F32, name="ctr_last", tag="y")
                 ctr_matmuls(ctr_last[:, :CHUNK_NODES], nodes)
-                nc.vector.tensor_tensor(e[:, nodes], peak[:, nodes], ctr_last[:, :CHUNK_NODES], ALU.add)
-                nc.vector.bn_stats(stats[:, c : c + 2, 0:3], e[:, nodes])
+                head_nodes = CHUNK_NODES - PIECE_NODES
+                parts = (slice(0, head_nodes), slice(head_nodes, CHUNK_NODES))
+                e_last = e[:, nodes]
+                peak_last = peak[:, nodes]
+                for part in parts:
+                    nc.vector.tensor_tensor(e_last[:, part], peak_last[:, part], ctr_last[:, part], ALU.add)
+                for i, part in enumerate(parts):
+                    nc.vector.bn_stats(stats[:, c + 2 * i : c + 2 * i + 2, 0:3], e_last[:, part])
 
         mean_var = held.tile([M, 2], F32, name="mean_var")
         nc.vector.bn_aggr(mean_var[:], stats[:, :, 0:3])

@@ -22,6 +22,7 @@ CHUNK_NODES = CHUNK_PIECES * PIECE_NODES
 SLOT = 8
 BLOCK = 256
 SCALAR_BLOCKS = 1
+CENTRED_BLOCKS = SCALAR_BLOCKS + 1
 WARM_MATMULS = 3
 QUARTER = 256
 EPS = 1e-5
@@ -54,11 +55,11 @@ def tile_spiralconvcombined_kernel(tc, x, w_nb, w_ctr, gamma, beta, offs, out):
         beta_sb = held.tile([M, 1], F32, name="beta_sb")
         nc.scalar.dma_start(beta_sb[:], beta)
 
-        zeros = held.tile([D, BANK], BF16, name="zeros")
-        nc.vector.memset(zeros[:].bitcast(F32), 0.0)
+        zeros = held.tile([D, M], BF16, name="zeros")
+        nc.gpsimd.memset(zeros[:].bitcast(F32), 0.0)
         warm = warm_bank.tile([M, BANK], F32, name="warm")
         for w in range(WARM_MATMULS):
-            nc.tensor.matmul(warm[:], zeros[:, :M], zeros[:], start=True, stop=True)
+            nc.tensor.matmul(warm[:], zeros[:], zeros[:, 0:1].to_broadcast([D, BANK]), start=True, stop=True)
 
         eps_sb = held.tile([M, 1], F32, name="eps_sb")
         nc.vector.memset(eps_sb[:], EPS)
@@ -130,6 +131,10 @@ def tile_spiralconvcombined_kernel(tc, x, w_nb, w_ctr, gamma, beta, offs, out):
         nc.vector.bn_aggr(mean_var[:], stats[:, :, 0:3])
         rstd = held.tile([M, 1], F32, name="rstd")
         nc.scalar.activation(rstd[:], mean_var[:, 1:2], ACT.Abs_reciprocal_sqrt, bias=eps_sb[:])
+        centred = held.tile([M, CENTRED_BLOCKS * BLOCK], F32, name="centred")
+        nc.vector.tensor_scalar(
+            centred[:], e[:, : CENTRED_BLOCKS * BLOCK], mean_var[:, 0:1], gamma_sb[:], ALU.subtract, ALU.mult
+        )
         neg_mean_gamma = held.tile([M, 1], F32, name="neg_mean_gamma")
         nc.vector.tensor_mul(neg_mean_gamma[:], mean_var[:, 0:1], neg_gamma[:])
         scale = held.tile([M, 1], F32, name="scale")
@@ -140,9 +145,17 @@ def tile_spiralconvcombined_kernel(tc, x, w_nb, w_ctr, gamma, beta, offs, out):
         result = held.tile([M, S], F32, name="result")
         for b in range(S // BLOCK):
             nodes = slice(b * BLOCK, (b + 1) * BLOCK)
+            if b < CENTRED_BLOCKS:
+                source, factor, addend = centred, rstd, beta_sb
+            else:
+                source, factor, addend = e, scale, shift
             if b < SCALAR_BLOCKS:
-                nc.scalar.activation(result[:, nodes], e[:, nodes], ACT.Identity, bias=shift[:], scale=scale[:])
+                nc.scalar.activation(
+                    result[:, nodes], source[:, nodes], ACT.Identity, bias=addend[:], scale=factor[:]
+                )
                 nc.scalar.dma_start(out[:, nodes], result[:, nodes])
             else:
-                nc.vector.tensor_scalar(result[:, nodes], e[:, nodes], scale[:], shift[:], ALU.mult, ALU.add)
+                nc.vector.tensor_scalar(
+                    result[:, nodes], source[:, nodes], factor[:], addend[:], ALU.mult, ALU.add
+                )
                 nc.sync.dma_start(out[:, nodes], result[:, nodes])

@@ -21,6 +21,7 @@ CHUNKS = N // (PIECE * CHUNK_PIECES)
 CHUNK_NODES = CHUNK_PIECES * PIECE_NODES
 SLOT = 8
 BLOCK = 256
+LAST_BLOCK = BLOCK // 2
 SCALAR_BLOCKS = 1
 CENTRED_BLOCKS = SCALAR_BLOCKS + 1
 WARM_MATMULS = 3
@@ -143,8 +144,9 @@ def tile_spiralconvcombined_kernel(tc, x, w_nb, w_ctr, gamma, beta, offs, out):
         nc.vector.tensor_scalar(shift[:], neg_mean_gamma[:], rstd[:], beta_sb[:], ALU.mult, ALU.add)
 
         result = held.tile([M, S], F32, name="result")
-        for b in range(S // BLOCK):
-            nodes = slice(b * BLOCK, (b + 1) * BLOCK)
+        starts = [0, BLOCK, 2 * BLOCK, S - LAST_BLOCK, S]
+        for b in range(len(starts) - 1):
+            nodes = slice(starts[b], starts[b + 1])
             if b < CENTRED_BLOCKS:
                 source, factor, addend = centred, rstd, beta_sb
             else:

import concourse.mybir as mybir

BF16 = mybir.dt.bfloat16
F32 = mybir.dt.float32
U16 = mybir.dt.uint16
ALU = mybir.AluOpType
ACT = mybir.ActivationFunctionType
AXIS_X = mybir.AxisListType.X

D = 128
M = 128
S = 1024
KN = 8
N = S * KN
PIECE = 512
PIECE_NODES = PIECE // KN
PIECE_COLS = PIECE // 16
BANK = 512
CHUNK_PIECES = 4
CHUNKS = N // (PIECE * CHUNK_PIECES)
CHUNK_NODES = CHUNK_PIECES * PIECE_NODES
SLOT = 8
BLOCK = 256
LAST_BLOCK = BLOCK // 2
SCALAR_BLOCKS = 1
CENTRED_BLOCKS = SCALAR_BLOCKS + 1
WARM_MATMULS = 3
QUARTER = 256
EPS = 1e-5

FLOPS = 2 * D * M * (N + 2 * S)


def tile_spiralconvcombined_kernel(tc, x, w_nb, w_ctr, gamma, beta, offs, out):
    nc = tc.nc
    with (
        tc.tile_pool(name="held", bufs=1) as held,
        tc.tile_pool(name="work", bufs=2) as work,
        tc.psum_pool(name="warm_bank", bufs=1) as warm_bank,
        tc.psum_pool(name="ctr_banks", bufs=1) as ctr_banks,
        tc.psum_pool(name="y_banks", bufs=5) as y_banks,
    ):
        w_nb_sb = held.tile([D, M], BF16, name="w_nb_sb")
        nc.sync.dma_start(w_nb_sb[:], w_nb)
        w_ctr_sb = held.tile([D, M], BF16, name="w_ctr_sb")
        nc.scalar.dma_start(w_ctr_sb[:], w_ctr)
        x_sb = held.tile([D, S], BF16, name="x_sb")
        for q in range(S // QUARTER):
            nodes = slice(q * QUARTER, (q + 1) * QUARTER)
            load_queue = nc.sync if q % 2 == 0 else nc.scalar
            load_queue.dma_start(x_sb[:, nodes], x[:, nodes])
        offsets = held.tile([128, N // 16], U16, name="offsets")
        nc.sync.dma_start(offsets[:], offs)
        gamma_sb = held.tile([M, 1], F32, name="gamma_sb")
        nc.scalar.dma_start(gamma_sb[:], gamma)
        beta_sb = held.tile([M, 1], F32, name="beta_sb")
        nc.scalar.dma_start(beta_sb[:], beta)

        zeros = held.tile([D, M], BF16, name="zeros")
        nc.gpsimd.memset(zeros[:].bitcast(F32), 0.0)
        warm = warm_bank.tile([M, BANK], F32, name="warm")
        for w in range(WARM_MATMULS):
            nc.tensor.matmul(warm[:], zeros[:], zeros[:, 0:1].to_broadcast([D, BANK]), start=True, stop=True)

        eps_sb = held.tile([M, 1], F32, name="eps_sb")
        nc.vector.memset(eps_sb[:], EPS)
        scratch = held.tile([M, 1], F32, name="scratch")
        nc.scalar.activation(scratch[:], eps_sb[:], ACT.Abs_reciprocal_sqrt)

        w_nb_neg = held.tile([D, M], BF16, name="w_nb_neg")
        nc.vector.tensor_scalar_mul(w_nb_neg[:], w_nb_sb[:], -1.0)
        def ctr_matmuls(ctr_cols, nodes):
            nc.tensor.matmul(ctr_cols, w_ctr_sb[:], x_sb[:, nodes], start=True, stop=False)
            nc.tensor.matmul(ctr_cols, w_nb_neg[:], x_sb[:, nodes], start=False, stop=True)

        early_nodes = (CHUNKS - 1) * CHUNK_NODES
        ctr_sb = held.tile([M, early_nodes], F32, name="ctr_sb")
        for first in range(0, early_nodes, BANK):
            width = min(BANK, early_nodes - first)
            ctr_ps = ctr_banks.tile([M, BANK], F32, name=f"ctr_ps{first // BANK}")
            for q in range(width // QUARTER):
                ctr_matmuls(
                    ctr_ps[:, q * QUARTER : (q + 1) * QUARTER],
                    slice(first + q * QUARTER, first + (q + 1) * QUARTER),
                )
            nc.scalar.copy(ctr_sb[:, first : first + width], ctr_ps[:, :width])

        neg_gamma = held.tile([M, 1], F32, name="neg_gamma")
        nc.gpsimd.tensor_scalar_mul(neg_gamma[:], gamma_sb[:], -1.0)

        peak = held.tile([M, S], F32, name="peak")
        e = held.tile([M, S], F32, name="e")
        stats = held.tile([M, CHUNKS + 3, SLOT], F32, name="stats")
        chunk_count = held.tile([M, CHUNKS - 1, 1], F32, name="chunk_count")
        nc.vector.memset(chunk_count[:], float(CHUNK_NODES))
        nc.scalar.copy(stats[:, : CHUNKS - 1, 0:1], chunk_count[:])
        for c in range(CHUNKS):
            for r in range(c * CHUNK_PIECES, (c + 1) * CHUNK_PIECES):
                y = y_banks.tile([M, PIECE], F32, name="y")
                piece = offsets[:, r * PIECE_COLS : (r + 1) * PIECE_COLS]
                nc.tensor.matmul(y[:], w_nb_sb[:], x_sb[:].indirect(piece), start=True, stop=True)
                nc.vector.tensor_reduce(
                    out=peak[:, r * PIECE_NODES : (r + 1) * PIECE_NODES],
                    in_=y[:].rearrange("m (n t) -> m n t", t=KN),
                    axis=AXIS_X,
                    op=ALU.max,
                )
            nodes = slice(c * CHUNK_NODES, (c + 1) * CHUNK_NODES)
            if c < CHUNKS - 1:
                nc.gpsimd.tensor_tensor(e[:, nodes], peak[:, nodes], ctr_sb[:, nodes], ALU.add)
                unused = work.tile([M, CHUNK_NODES], F32, name="unused")
                total = work.tile([M, 1], F32, name="total")
                nc.scalar.activation(unused[:], e[:, nodes], ACT.Identity, accum_out=total[:])
                nc.scalar.mul(stats[:, c, 1:2], total[:], 1.0 / CHUNK_NODES)
                nc.scalar.activation(
                    unused[:], e[:, nodes], ACT.Square,
                    bias=stats[:, c, 1:2], scale=-1.0, accum_out=stats[:, c, 2:3],
                )
            else:
                ctr_last = y_banks.tile([M, PIECE], F32, name="ctr_last", tag="y")
                ctr_matmuls(ctr_last[:, :CHUNK_NODES], nodes)
                head_nodes = CHUNK_NODES - PIECE_NODES
                parts = (slice(0, head_nodes), slice(head_nodes, CHUNK_NODES))
                e_last = e[:, nodes]
                peak_last = peak[:, nodes]
                for part in parts:
                    nc.vector.tensor_tensor(e_last[:, part], peak_last[:, part], ctr_last[:, part], ALU.add)
                for i, part in enumerate(parts):
                    nc.vector.bn_stats(stats[:, c + 2 * i : c + 2 * i + 2, 0:3], e_last[:, part])

        mean_var = held.tile([M, 2], F32, name="mean_var")
        nc.vector.bn_aggr(mean_var[:], stats[:, :, 0:3])
        rstd = held.tile([M, 1], F32, name="rstd")
        nc.scalar.activation(rstd[:], mean_var[:, 1:2], ACT.Abs_reciprocal_sqrt, bias=eps_sb[:])
        centred = held.tile([M, CENTRED_BLOCKS * BLOCK], F32, name="centred")
        nc.vector.tensor_scalar(
            centred[:], e[:, : CENTRED_BLOCKS * BLOCK], mean_var[:, 0:1], gamma_sb[:], ALU.subtract, ALU.mult
        )
        neg_mean_gamma = held.tile([M, 1], F32, name="neg_mean_gamma")
        nc.vector.tensor_mul(neg_mean_gamma[:], mean_var[:, 0:1], neg_gamma[:])
        scale = held.tile([M, 1], F32, name="scale")
        nc.vector.tensor_mul(scale[:], gamma_sb[:], rstd[:])
        shift = held.tile([M, 1], F32, name="shift")
        nc.vector.tensor_scalar(shift[:], neg_mean_gamma[:], rstd[:], beta_sb[:], ALU.mult, ALU.add)

        result = held.tile([M, S], F32, name="result")
        starts = [0, BLOCK, 2 * BLOCK, S - LAST_BLOCK, S]
        for b in range(len(starts) - 1):
            nodes = slice(starts[b], starts[b + 1])
            if b < CENTRED_BLOCKS:
                source, factor, addend = centred, rstd, beta_sb
            else:
                source, factor, addend = e, scale, shift
            if b < SCALAR_BLOCKS:
                nc.scalar.activation(
                    result[:, nodes], source[:, nodes], ACT.Identity, bias=addend[:], scale=factor[:]
                )
                nc.scalar.dma_start(out[:, nodes], result[:, nodes])
            else:
                nc.vector.tensor_scalar(
                    result[:, nodes], source[:, nodes], factor[:], addend[:], ALU.mult, ALU.add
                )
                nc.sync.dma_start(out[:, nodes], result[:, nodes])
